import numpy as np
import ml_dtypes


def mxq(x, axis, fmt="e4m3"):
    dtype, down = {"e4m3": (ml_dtypes.float8_e4m3fn, 7), "e5m2": (ml_dtypes.float8_e5m2, 14)}[fmt]
    v = np.moveaxis(np.asarray(x, np.float32).astype(ml_dtypes.bfloat16).astype(np.float64), axis, -1)
    blocks = v.reshape(v.shape[:-1] + (-1, 32))
    amax = np.abs(blocks).max(-1, keepdims=True)
    byte = np.maximum(np.where(amax > 0, np.frexp(amax)[1] - 1 + 127, 0) - down, 1)
    scale = np.exp2(byte - 127.0)
    codes = (blocks / scale).astype(np.float32).astype(dtype).astype(np.float64)
    return np.moveaxis((codes * scale).reshape(v.shape), -1, axis)


WIDE = False


def mx_kscale(k):
    if not WIDE:
        return np.ones(k)
    levels = np.array([10, -10, 5, -5, 0])
    a = np.random.permutation(np.resize(levels, k // 512 * 4)).reshape(k // 512, 4)
    idx = np.arange(k)
    return np.exp2(a[idx // 512, idx % 128 // 32])


BF16 = ml_dtypes.bfloat16


def bf(x):
    return np.asarray(x, np.float32).astype(BF16)


def f64(x):
    return np.asarray(x).astype(np.float64)


E2M1 = np.array([0.0, 0.5, 1.0, 1.5, 2.0, 3.0, 4.0, 6.0, -0.0, -0.5, -1.0, -1.5, -2.0, -3.0, -4.0, -6.0])


def pack_weight(w, fmt):
    k, n = w.shape
    w = f64(bf(w)).reshape(k // 32, 32, n)
    amax = np.abs(w).max(1)
    if fmt == "e4m3":
        byte = np.frexp(amax)[1] - 1 + 127 - 7
    else:
        mant, ex = np.frexp(amax / 6.0)
        byte = np.where(mant > 0.5, ex, ex - 1) + 127
    byte = np.clip(np.where(amax > 0, byte, 1), 1, 254)
    scaled = (w * np.exp2(127.0 - byte)[:, None, :]).reshape(k, n).astype(np.float32)
    by_word = np.ascontiguousarray(scaled.reshape(k // 512, 128, 4, n).transpose(0, 1, 3, 2))
    if fmt == "e4m3":
        words = by_word.astype(ml_dtypes.float8_e4m3fn).view(np.uint8)
    else:
        c = by_word.astype(ml_dtypes.float4_e2m1fn).view(np.uint8) & 0xF
        words = c[..., 0::2] | (c[..., 1::2] << 4)
    return np.ascontiguousarray(words), np.ascontiguousarray(byte.astype(np.uint8).reshape(k // 512, 16, n))


def unpack_weight(words, scales, fmt):
    g, p, n, _ = words.shape
    if fmt == "e4m3":
        vals = np.ascontiguousarray(words).view(ml_dtypes.float8_e4m3fn).astype(np.float64)
    else:
        nib = np.empty((g, p, n, 4), np.uint8)
        nib[..., 0::2] = words & 0xF
        nib[..., 1::2] = words >> 4
        vals = E2M1[nib]
    vals = vals * np.repeat(np.exp2(scales.astype(np.float64) - 127.0), 8, axis=1)[..., None]
    return vals.transpose(0, 1, 3, 2).reshape(g * 512, n)


B, I, H = 128, 15872, 512
C = I + H
FMT = "e4m3"


def hard_sigmoid(v):
    return np.clip(v / 6.0 + 0.5, 0.0, 1.0)


def hard_tanh(v):
    return np.clip(v, -1.0, 1.0)


def setup_inputs():
    s = np.where(np.arange(C) < I, mx_kscale(C), 1.0)
    inputs = bf(np.random.standard_normal((B, I)) * s[:I])
    h_prev = bf(np.random.standard_normal((B, H)))
    W_z_words, W_z_scales = pack_weight(np.ascontiguousarray((np.random.standard_normal((H, C)) * 2.5 / np.sqrt(C) / s).T), FMT)
    b_z = bf(np.random.standard_normal(H) * 1.0)
    W_r_words, W_r_scales = pack_weight(np.ascontiguousarray((np.random.standard_normal((H, C)) * 2.5 / np.sqrt(C) / s).T), FMT)
    b_r = bf(np.random.standard_normal(H) * 1.0)
    W_h_words, W_h_scales = pack_weight(np.ascontiguousarray((np.random.standard_normal((H, C)) * 1.2 / np.sqrt(C) / s).T), FMT)
    b_h = bf(np.random.standard_normal(H) * 0.5)
    return {"inputs": inputs,
            "h_prev": h_prev,
            "W_z_words": W_z_words,
            "W_z_scales": W_z_scales,
            "b_z": b_z,
            "W_r_words": W_r_words,
            "W_r_scales": W_r_scales,
            "b_r": b_r,
            "W_h_words": W_h_words,
            "W_h_scales": W_h_scales,
            "b_h": b_h}


def reference(inputs, h_prev, W_z_words, W_z_scales, b_z, W_r_words, W_r_scales, b_r, W_h_words, W_h_scales, b_h):
    h = f64(h_prev)
    xq = mxq(f64(inputs), 1, "e4m3")
    ihq = np.concatenate([xq, mxq(h, 1, "e4m3")], axis=-1)
    z = hard_sigmoid((ihq @ unpack_weight(W_z_words, W_z_scales, FMT)) + f64(b_z))
    r = hard_sigmoid((ihq @ unpack_weight(W_r_words, W_r_scales, FMT)) + f64(b_r))
    irhq = np.concatenate([xq, mxq(r * h, 1, "e4m3")], axis=-1)
    h_tilde = hard_tanh((irhq @ unpack_weight(W_h_words, W_h_scales, FMT)) + f64(b_h))
    return z * h + (1.0 - z) * h_tilde

@@ -1,0 +1,244 @@
+from contextlib import ExitStack
+
+import concourse.mybir as mybir
+from concourse.masks import make_identity
+
+F32 = mybir.dt.float32
+BF16 = mybir.dt.bfloat16
+I32 = mybir.dt.int32
+U32 = mybir.dt.uint32
+U8 = mybir.dt.uint8
+FP8X4 = mybir.dt.float8_e4m3fn_x4
+ALU = mybir.AluOpType
+
+P = 128
+PACK = 4
+K_PASS = P * PACK
+BATCH = 128
+IN_FEATURES = 15872
+HIDDEN = 512
+FEATURES = IN_FEATURES + HIDDEN
+PASSES = FEATURES // K_PASS
+PAIRS_PER_PASS = K_PASS // 2
+
+PASSES_PER_BANK = 2
+BANKS_PER_ROUND = 2
+PASSES_PER_ROUND = PASSES_PER_BANK * BANKS_PER_ROUND
+PASSES_PER_X_LOAD = 8
+PASSES_PER_W_LOAD = 4
+W_BUFFERS = 12
+
+PLANES_PER_TILE = 4
+SLOTS = PASSES // PLANES_PER_TILE
+
+FLOPS = 3 * 2 * BATCH * FEATURES * HIDDEN
+
+
+def load_weight_scales(nc, planes, scales):
+    scales_f32 = scales.bitcast(F32)
+    for o in range(PLANES_PER_TILE):
+        for quadrant in range(4):
+            rows = slice(32 * quadrant + 4 * o, 32 * quadrant + 4 * o + 4)
+            nc.gpsimd.dma_start(
+                out=planes[rows, :, :].bitcast(F32),
+                in_=scales_f32[
+                    SLOTS * o : SLOTS * (o + 1), 4 * quadrant : 4 * quadrant + 4, :
+                ].rearrange("s r n -> r s n"),
+            )
+
+
+def gate_matmul(nc, w_pool, acc, words, planes, act_codes, act_scales):
+    words_i32 = words.rearrange("g p n t -> p g (n t)").bitcast(I32)
+    for first in range(0, PASSES, PASSES_PER_W_LOAD):
+        w = w_pool.tile([P, PASSES_PER_W_LOAD, HIDDEN], U32, align_bytes=64)
+        nc.sync.dma_start(
+            out=w[:].bitcast(I32), in_=words_i32[:, first : first + PASSES_PER_W_LOAD, :]
+        )
+        for j in range(PASSES_PER_W_LOAD):
+            g = first + j
+            nc.tensor.matmul_mx(
+                out=acc[:],
+                lhsT=act_codes[g].bitcast(FP8X4),
+                lhsT_scale=act_scales[g],
+                rhs=w[:, j, :].bitcast(FP8X4),
+                rhs_scale=planes[4 * (g // SLOTS) : P, g % SLOTS, :],
+                start=(g == 0),
+                stop=(g == PASSES - 1),
+            )
+
+
+def hard_sigmoid(nc, gate, acc, offset):
+    nc.vector.scalar_tensor_tensor(
+        out=gate[:], in0=acc[:], scalar=1.0 / 6.0, in1=offset[:], op0=ALU.mult, op1=ALU.add
+    )
+    nc.vector.tensor_scalar(
+        out=gate[:], in0=gate[:], scalar1=0.0, scalar2=1.0, op0=ALU.max, op1=ALU.min
+    )
+
+
+def tile_grucell_k_kernel(
+    tc,
+    inputs,
+    h_prev,
+    W_z_words,
+    W_z_scales,
+    b_z,
+    W_r_words,
+    W_r_scales,
+    b_r,
+    W_h_words,
+    W_h_scales,
+    b_h,
+    out,
+):
+    nc = tc.nc
+    with ExitStack() as ctx:
+        keep = ctx.enter_context(tc.tile_pool(name="keep", bufs=1))
+        stage = ctx.enter_context(tc.tile_pool(name="stage", bufs=3))
+        w_pool = ctx.enter_context(tc.tile_pool(name="weights", bufs=W_BUFFERS))
+        psum_t = ctx.enter_context(tc.psum_pool(name="psum_t", bufs=3))
+        psum_b = ctx.enter_context(tc.psum_pool(name="psum_b", bufs=2))
+        psum_acc = ctx.enter_context(tc.psum_pool(name="psum_acc", bufs=1))
+
+        ident_f32 = keep.tile([P, P], F32)
+        make_identity(nc, ident_f32[:])
+        ident_bf16 = keep.tile([P, P], BF16)
+        make_identity(nc, ident_bf16[:])
+
+        planes_r = keep.tile([P, SLOTS, HIDDEN], U8, align_bytes=64)
+        planes_z = keep.tile([P, SLOTS, HIDDEN], U8, align_bytes=64)
+        planes_h = keep.tile([P, SLOTS, HIDDEN], U8, align_bytes=64)
+        nc.vector.memset(planes_r[:].bitcast(I32), 0)
+        load_weight_scales(nc, planes_r, W_r_scales)
+
+        bias_rows = keep.tile([P, 3 * HIDDEN], BF16)
+        nc.vector.memset(bias_rows[:], 0.0)
+        for i, bias in enumerate((b_r, b_z, b_h)):
+            nc.scalar.dma_start(
+                out=bias_rows[0:1, i * HIDDEN : (i + 1) * HIDDEN], in_=bias.unsqueeze(0)
+            )
+        ones = keep.tile([P, P], BF16)
+        nc.vector.memset(ones[:], 1.0)
+
+        nc.vector.memset(planes_z[:].bitcast(I32), 0)
+        load_weight_scales(nc, planes_z, W_z_scales)
+        nc.vector.memset(planes_h[:].bitcast(I32), 0)
+        load_weight_scales(nc, planes_h, W_h_scales)
+
+        ih = keep.tile([P, FEATURES], BF16)
+        x_load = PASSES_PER_X_LOAD * K_PASS
+        for first in range(0, IN_FEATURES, x_load):
+            cols = slice(first, min(first + x_load, IN_FEATURES))
+            nc.sync.dma_start(out=ih[:, cols], in_=inputs[:, cols])
+        h = ih[:, IN_FEATURES:FEATURES]
+        nc.sync.dma_start(out=h, in_=h_prev)
+
+        offset_r = keep.tile([P, HIDDEN], F32)
+        offset_z = keep.tile([P, HIDDEN], F32)
+        bias_h = keep.tile([P, HIDDEN], F32)
+        spreads = ((offset_r, 1.0 / 6.0, 0.5), (offset_z, 1.0 / 6.0, 0.5), (bias_h, 1.0, 0.0))
+        for i, (spread, factor, shift) in enumerate(spreads):
+            bias_ps = psum_b.tile([P, HIDDEN], F32)
+            nc.tensor.matmul(
+                bias_ps[:],
+                lhsT=ones[:],
+                rhs=bias_rows[:, i * HIDDEN : (i + 1) * HIDDEN],
+                start=True,
+                stop=True,
+            )
+            nc.vector.tensor_scalar(
+                out=spread[:],
+                in0=bias_ps[:],
+                scalar1=factor,
+                scalar2=shift,
+                op0=ALU.mult,
+                op1=ALU.add,
+            )
+
+        ih_codes = keep.tile([P, PASSES * BATCH], U32, align_bytes=64)
+        ih_scales = keep.tile([P, PASSES * BATCH], U8, align_bytes=64)
+        ih_pairs = ih[:].bitcast(F32)
+        for first in range(0, PASSES, PASSES_PER_ROUND):
+            grouped = stage.tile([P, PASSES_PER_ROUND * BATCH * PACK], BF16, align_bytes=64)
+            grouped_pairs = (
+                grouped[:].bitcast(F32).rearrange("p (g b u) -> p g b u", g=PASSES_PER_ROUND, u=2)
+            )
+            for bank in range(BANKS_PER_ROUND):
+                pairs_t = psum_t.tile([P, PASSES_PER_BANK, 2, BATCH], F32, tag="transposed")
+                for i in range(PASSES_PER_BANK):
+                    g = first + bank * PASSES_PER_BANK + i
+                    for u in range(2):
+                        nc.tensor.transpose(
+                            pairs_t[:, i, u, :],
+                            ih_pairs[:, PAIRS_PER_PASS * g + u : PAIRS_PER_PASS * (g + 1) : 2],
+                            ident_f32[:],
+                        )
+                copy = nc.vector.tensor_copy if bank % 2 == 0 else nc.scalar.copy
+                copy(
+                    out=grouped_pairs[
+                        :, bank * PASSES_PER_BANK : (bank + 1) * PASSES_PER_BANK, :, :
+                    ],
+                    in_=pairs_t[:].rearrange("p g u b -> p g b u"),
+                )
+            cols = slice(first * BATCH, (first + PASSES_PER_ROUND) * BATCH)
+            nc.vector.quantize_mx(
+                out=ih_codes[:, cols].bitcast(FP8X4), scales=ih_scales[:, cols], in_=grouped[:]
+            )
+        ih_codes_by_pass = [ih_codes[:, g * BATCH : (g + 1) * BATCH] for g in range(PASSES)]
+        ih_scales_by_pass = [ih_scales[:, g * BATCH : (g + 1) * BATCH] for g in range(PASSES)]
+
+        acc_r = psum_acc.tile([P, HIDDEN], F32)
+        gate_matmul(nc, w_pool, acc_r, W_r_words, planes_r, ih_codes_by_pass, ih_scales_by_pass)
+        r = keep.tile([P, HIDDEN], F32)
+        hard_sigmoid(nc, r, acc_r, offset_r)
+
+        rh_sorted = keep.tile([P, PACK, P], BF16)
+        nc.vector.tensor_tensor(
+            out=rh_sorted[:],
+            in0=r[:].rearrange("b (p t) -> b t p", t=PACK),
+            in1=h.rearrange("b (p t) -> b t p", t=PACK),
+            op=ALU.mult,
+        )
+
+        acc_z = psum_acc.tile([P, HIDDEN], F32)
+        gate_matmul(nc, w_pool, acc_z, W_z_words, planes_z, ih_codes_by_pass, ih_scales_by_pass)
+        z = keep.tile([P, HIDDEN], F32)
+        hard_sigmoid(nc, z, acc_z, offset_z)
+        zh = keep.tile([P, HIDDEN], F32)
+        nc.vector.tensor_tensor(out=zh[:], in0=z[:], in1=h, op=ALU.mult)
+        one_minus_z = keep.tile([P, HIDDEN], F32)
+        nc.vector.tensor_scalar(
+            out=one_minus_z[:], in0=z[:], scalar1=-1.0, scalar2=1.0, op0=ALU.mult, op1=ALU.add
+        )
+
+        rh_t = psum_t.tile([P, PACK, BATCH], BF16, tag="transposed")
+        for t in range(PACK):
+            nc.tensor.transpose(rh_t[:, t, :], rh_sorted[:, t, :], ident_bf16[:])
+        rh_grouped = keep.tile([P, BATCH, PACK], BF16, align_bytes=64)
+        nc.vector.tensor_copy(out=rh_grouped[:], in_=rh_t[:].rearrange("p t b -> p b t"))
+        rh_codes = keep.tile([P, BATCH], U32, align_bytes=64)
+        rh_scales = keep.tile([P, BATCH], U8, align_bytes=64)
+        nc.vector.quantize_mx(
+            out=rh_codes[:].bitcast(FP8X4),
+            scales=rh_scales[:],
+            in_=rh_grouped[:].rearrange("p b t -> p (b t)"),
+        )
+
+        acc_h = psum_acc.tile([P, HIDDEN], F32)
+        gate_matmul(
+            nc,
+            w_pool,
+            acc_h,
+            W_h_words,
+            planes_h,
+            ih_codes_by_pass[: PASSES - 1] + [rh_codes[:]],
+            ih_scales_by_pass[: PASSES - 1] + [rh_scales[:]],
+        )
+        y = keep.tile([P, HIDDEN], F32)
+        nc.vector.tensor_tensor(out=y[:], in0=acc_h[:], in1=bias_h[:], op=ALU.add)
+        nc.vector.tensor_scalar(
+            out=y[:], in0=y[:], scalar1=-1.0, scalar2=1.0, op0=ALU.max, op1=ALU.min
+        )
+        nc.vector.tensor_tensor(out=y[:], in0=y[:], in1=one_minus_z[:], op=ALU.mult)
+        nc.vector.tensor_tensor(out=y[:], in0=y[:], in1=zh[:], op=ALU.add)
+        nc.sync.dma_start(out=out, in_=y[:])

@@ -24,27 +24,23 @@ PAIRS_PER_PASS = K_PASS // 2
 PASSES_PER_BANK = 2
 BANKS_PER_ROUND = 2
 PASSES_PER_ROUND = PASSES_PER_BANK * BANKS_PER_ROUND
-PASSES_PER_X_LOAD = 8
+ROUNDS = PASSES // PASSES_PER_ROUND
 PASSES_PER_W_LOAD = 4
 W_BUFFERS = 12
 
 PLANES_PER_TILE = 4
 SLOTS = PASSES // PLANES_PER_TILE
+BLOCKS_PER_PASS = K_PASS // 32
 
 FLOPS = 3 * 2 * BATCH * FEATURES * HIDDEN
 
 
-def load_weight_scales(nc, planes, scales):
-    scales_f32 = scales.bitcast(F32)
-    for o in range(PLANES_PER_TILE):
-        for quadrant in range(4):
-            rows = slice(32 * quadrant + 4 * o, 32 * quadrant + 4 * o + 4)
-            nc.gpsimd.dma_start(
-                out=planes[rows, :, :].bitcast(F32),
-                in_=scales_f32[
-                    SLOTS * o : SLOTS * (o + 1), 4 * quadrant : 4 * quadrant + 4, :
-                ].rearrange("s r n -> r s n"),
-            )
+def load_scale_row(queue, view, planes, scales, q):
+    quadrant, r = divmod(q, 4)
+    queue.dma_start(
+        out=planes[32 * quadrant + r : 32 * quadrant + 4 * PLANES_PER_TILE : 4, :, :].bitcast(view),
+        in_=scales.bitcast(view)[:, q, :].rearrange("(o s) n -> o s n", o=PLANES_PER_TILE),
+    )
 
 
 def gate_matmul(nc, w_pool, acc, words, planes, act_codes, act_scales):
@@ -94,6 +90,7 @@ def tile_grucell_k_kernel(
     nc = tc.nc
     with ExitStack() as ctx:
         keep = ctx.enter_context(tc.tile_pool(name="keep", bufs=1))
+        ih_pool = ctx.enter_context(tc.tile_pool(name="ih", bufs=ROUNDS))
         stage = ctx.enter_context(tc.tile_pool(name="stage", bufs=3))
         w_pool = ctx.enter_context(tc.tile_pool(name="weights", bufs=W_BUFFERS))
         psum_t = ctx.enter_context(tc.psum_pool(name="psum_t", bufs=3))
@@ -109,7 +106,6 @@ def tile_grucell_k_kernel(
         planes_z = keep.tile([P, SLOTS, HIDDEN], U8, align_bytes=64)
         planes_h = keep.tile([P, SLOTS, HIDDEN], U8, align_bytes=64)
         nc.vector.memset(planes_r[:].bitcast(I32), 0)
-        load_weight_scales(nc, planes_r, W_r_scales)
 
         bias_rows = keep.tile([P, 3 * HIDDEN], BF16)
         nc.vector.memset(bias_rows[:], 0.0)
@@ -121,17 +117,27 @@ def tile_grucell_k_kernel(
         nc.vector.memset(ones[:], 1.0)
 
         nc.vector.memset(planes_z[:].bitcast(I32), 0)
-        load_weight_scales(nc, planes_z, W_z_scales)
         nc.vector.memset(planes_h[:].bitcast(I32), 0)
-        load_weight_scales(nc, planes_h, W_h_scales)
+        for q in range(BLOCKS_PER_PASS):
+            load_scale_row(nc.gpsimd, F32, planes_z, W_z_scales, q)
+        for q in range(BLOCKS_PER_PASS):
+            load_scale_row(nc.gpsimd, F32, planes_h, W_h_scales, q)
 
-        ih = keep.tile([P, FEATURES], BF16)
-        x_load = PASSES_PER_X_LOAD * K_PASS
-        for first in range(0, IN_FEATURES, x_load):
-            cols = slice(first, min(first + x_load, IN_FEATURES))
-            nc.sync.dma_start(out=ih[:, cols], in_=inputs[:, cols])
-        h = ih[:, IN_FEATURES:FEATURES]
-        nc.sync.dma_start(out=h, in_=h_prev)
+        part_k = PASSES_PER_ROUND * K_PASS
+        rows_per_part = BLOCKS_PER_PASS // ROUNDS
+        ih_parts = []
+        for i in range(ROUNDS):
+            part = ih_pool.tile([P, part_k], BF16, tag="ih")
+            from_inputs = min(part_k, IN_FEATURES - i * part_k)
+            nc.sync.dma_start(
+                out=part[:, 0:from_inputs], in_=inputs[:, i * part_k : i * part_k + from_inputs]
+            )
+            if from_inputs < part_k:
+                nc.sync.dma_start(out=part[:, from_inputs:part_k], in_=h_prev)
+            for q in range(i * rows_per_part, (i + 1) * rows_per_part):
+                load_scale_row(nc.sync, I32, planes_r, W_r_scales, q)
+            ih_parts.append(part)
+        h = ih_parts[ROUNDS - 1][:, part_k - HIDDEN : part_k]
 
         offset_r = keep.tile([P, HIDDEN], F32)
         offset_z = keep.tile([P, HIDDEN], F32)
@@ -157,8 +163,8 @@ def tile_grucell_k_kernel(
 
         ih_codes = keep.tile([P, PASSES * BATCH], U32, align_bytes=64)
         ih_scales = keep.tile([P, PASSES * BATCH], U8, align_bytes=64)
-        ih_pairs = ih[:].bitcast(F32)
-        for first in range(0, PASSES, PASSES_PER_ROUND):
+        for rnd in range(ROUNDS):
+            ih_pairs = ih_parts[rnd][:].bitcast(F32)
             grouped = stage.tile([P, PASSES_PER_ROUND * BATCH * PACK], BF16, align_bytes=64)
             grouped_pairs = (
                 grouped[:].bitcast(F32).rearrange("p (g b u) -> p g b u", g=PASSES_PER_ROUND, u=2)
@@ -166,7 +172,7 @@ def tile_grucell_k_kernel(
             for bank in range(BANKS_PER_ROUND):
                 pairs_t = psum_t.tile([P, PASSES_PER_BANK, 2, BATCH], F32, tag="transposed")
                 for i in range(PASSES_PER_BANK):
-                    g = first + bank * PASSES_PER_BANK + i
+                    g = bank * PASSES_PER_BANK + i
                     for u in range(2):
                         nc.tensor.transpose(
                             pairs_t[:, i, u, :],
@@ -180,7 +186,7 @@ def tile_grucell_k_kernel(
                     ],
                     in_=pairs_t[:].rearrange("p g u b -> p g b u"),
                 )
-            cols = slice(first * BATCH, (first + PASSES_PER_ROUND) * BATCH)
+            cols = slice(rnd * PASSES_PER_ROUND * BATCH, (rnd + 1) * PASSES_PER_ROUND * BATCH)
             nc.vector.quantize_mx(
                 out=ih_codes[:, cols].bitcast(FP8X4), scales=ih_scales[:, cols], in_=grouped[:]
             )

@@ -35,21 +35,26 @@ BLOCKS_PER_PASS = K_PASS // 32
 FLOPS = 3 * 2 * BATCH * FEATURES * HIDDEN
 
 
-def load_scale_row(queue, view, planes, scales, q):
+def load_scale_row(nc, planes, scales, q):
     quadrant, r = divmod(q, 4)
-    queue.dma_start(
-        out=planes[32 * quadrant + r : 32 * quadrant + 4 * PLANES_PER_TILE : 4, :, :].bitcast(view),
-        in_=scales.bitcast(view)[:, q, :].rearrange("(o s) n -> o s n", o=PLANES_PER_TILE),
+    nc.sync.dma_start(
+        out=planes[32 * quadrant + r : 32 * quadrant + 4 * PLANES_PER_TILE : 4, :, :].bitcast(I32),
+        in_=scales.bitcast(I32)[:, q, :].rearrange("(o s) n -> o s n", o=PLANES_PER_TILE),
     )
 
 
-def gate_matmul(nc, w_pool, acc, words, planes, act_codes, act_scales):
+def gate_matmul(nc, w_pool, acc, words, planes, act_codes, act_scales, next_planes, next_scales):
     words_i32 = words.rearrange("g p n t -> p g (n t)").bitcast(I32)
+    rows_per_load = BLOCKS_PER_PASS * PASSES_PER_W_LOAD // PASSES
     for first in range(0, PASSES, PASSES_PER_W_LOAD):
         w = w_pool.tile([P, PASSES_PER_W_LOAD, HIDDEN], U32, align_bytes=64)
         nc.sync.dma_start(
             out=w[:].bitcast(I32), in_=words_i32[:, first : first + PASSES_PER_W_LOAD, :]
         )
+        if next_scales is not None:
+            load = first // PASSES_PER_W_LOAD
+            for q in range(load * rows_per_load, (load + 1) * rows_per_load):
+                load_scale_row(nc, next_planes, next_scales, q)
         for j in range(PASSES_PER_W_LOAD):
             g = first + j
             nc.tensor.matmul_mx(
@@ -118,10 +123,6 @@ def tile_grucell_k_kernel(
 
         nc.vector.memset(planes_z[:].bitcast(I32), 0)
         nc.vector.memset(planes_h[:].bitcast(I32), 0)
-        for q in range(BLOCKS_PER_PASS):
-            load_scale_row(nc.gpsimd, F32, planes_z, W_z_scales, q)
-        for q in range(BLOCKS_PER_PASS):
-            load_scale_row(nc.gpsimd, F32, planes_h, W_h_scales, q)
 
         part_k = PASSES_PER_ROUND * K_PASS
         rows_per_part = BLOCKS_PER_PASS // ROUNDS
@@ -135,7 +136,7 @@ def tile_grucell_k_kernel(
             if from_inputs < part_k:
                 nc.sync.dma_start(out=part[:, from_inputs:part_k], in_=h_prev)
             for q in range(i * rows_per_part, (i + 1) * rows_per_part):
-                load_scale_row(nc.sync, I32, planes_r, W_r_scales, q)
+                load_scale_row(nc, planes_r, W_r_scales, q)
             ih_parts.append(part)
         h = ih_parts[ROUNDS - 1][:, part_k - HIDDEN : part_k]
 
@@ -194,7 +195,17 @@ def tile_grucell_k_kernel(
         ih_scales_by_pass = [ih_scales[:, g * BATCH : (g + 1) * BATCH] for g in range(PASSES)]
 
         acc_r = psum_acc.tile([P, HIDDEN], F32)
-        gate_matmul(nc, w_pool, acc_r, W_r_words, planes_r, ih_codes_by_pass, ih_scales_by_pass)
+        gate_matmul(
+            nc,
+            w_pool,
+            acc_r,
+            W_r_words,
+            planes_r,
+            ih_codes_by_pass,
+            ih_scales_by_pass,
+            planes_z,
+            W_z_scales,
+        )
         r = keep.tile([P, HIDDEN], F32)
         hard_sigmoid(nc, r, acc_r, offset_r)
 
@@ -207,7 +218,17 @@ def tile_grucell_k_kernel(
         )
 
         acc_z = psum_acc.tile([P, HIDDEN], F32)
-        gate_matmul(nc, w_pool, acc_z, W_z_words, planes_z, ih_codes_by_pass, ih_scales_by_pass)
+        gate_matmul(
+            nc,
+            w_pool,
+            acc_z,
+            W_z_words,
+            planes_z,
+            ih_codes_by_pass,
+            ih_scales_by_pass,
+            planes_h,
+            W_h_scales,
+        )
         z = keep.tile([P, HIDDEN], F32)
         hard_sigmoid(nc, z, acc_z, offset_z)
         zh = keep.tile([P, HIDDEN], F32)
@@ -239,6 +260,8 @@ def tile_grucell_k_kernel(
             planes_h,
             ih_codes_by_pass[: PASSES - 1] + [rh_codes[:]],
             ih_scales_by_pass[: PASSES - 1] + [rh_scales[:]],
+            None,
+            None,
         )
         y = keep.tile([P, HIDDEN], F32)
         nc.vector.tensor_tensor(out=y[:], in0=acc_h[:], in1=bias_h[:], op=ALU.add)

@@ -35,27 +35,24 @@ BLOCKS_PER_PASS = K_PASS // 32
 FLOPS = 3 * 2 * BATCH * FEATURES * HIDDEN
 
 
-def load_scale_row(nc, planes, scales, q):
+def load_scale_row(queue, view, planes, scales, q):
     quadrant, r = divmod(q, 4)
-    nc.sync.dma_start(
-        out=planes[32 * quadrant + r : 32 * quadrant + 4 * PLANES_PER_TILE : 4, :, :].bitcast(I32),
-        in_=scales.bitcast(I32)[:, q, :].rearrange("(o s) n -> o s n", o=PLANES_PER_TILE),
+    queue.dma_start(
+        out=planes[32 * quadrant + r : 32 * quadrant + 4 * PLANES_PER_TILE : 4, :, :].bitcast(view),
+        in_=scales.bitcast(view)[:, q, :].rearrange("(o s) n -> o s n", o=PLANES_PER_TILE),
     )
 
 
-def gate_matmul(nc, w_pool, acc, words, planes, act_codes, act_scales, next_planes, next_scales):
+def gate_matmul(nc, w_pool, acc, words, planes, act_codes, act_scales, fine_end):
     words_i32 = words.rearrange("g p n t -> p g (n t)").bitcast(I32)
-    rows_per_load = BLOCKS_PER_PASS * PASSES_PER_W_LOAD // PASSES
-    for first in range(0, PASSES, PASSES_PER_W_LOAD):
-        w = w_pool.tile([P, PASSES_PER_W_LOAD, HIDDEN], U32, align_bytes=64)
-        nc.sync.dma_start(
-            out=w[:].bitcast(I32), in_=words_i32[:, first : first + PASSES_PER_W_LOAD, :]
-        )
-        if next_scales is not None:
-            load = first // PASSES_PER_W_LOAD
-            for q in range(load * rows_per_load, (load + 1) * rows_per_load):
-                load_scale_row(nc, next_planes, next_scales, q)
-        for j in range(PASSES_PER_W_LOAD):
+    load_sizes = [PASSES_PER_W_LOAD] * (PASSES // PASSES_PER_W_LOAD)
+    if fine_end:
+        load_sizes = load_sizes[:-1] + [1] * PASSES_PER_W_LOAD
+    first = 0
+    for size in load_sizes:
+        w = w_pool.tile([P, size, HIDDEN], U32, tag="w", align_bytes=64)
+        nc.sync.dma_start(out=w[:].bitcast(I32), in_=words_i32[:, first : first + size, :])
+        for j in range(size):
             g = first + j
             nc.tensor.matmul_mx(
                 out=acc[:],
@@ -66,6 +63,7 @@ def gate_matmul(nc, w_pool, acc, words, planes, act_codes, act_scales, next_plan
                 start=(g == 0),
                 stop=(g == PASSES - 1),
             )
+        first += size
 
 
 def hard_sigmoid(nc, gate, acc, offset):
@@ -104,13 +102,13 @@ def tile_grucell_k_kernel(
 
         ident_f32 = keep.tile([P, P], F32)
         make_identity(nc, ident_f32[:])
-        ident_bf16 = keep.tile([P, P], BF16)
-        make_identity(nc, ident_bf16[:])
 
         planes_r = keep.tile([P, SLOTS, HIDDEN], U8, align_bytes=64)
         planes_z = keep.tile([P, SLOTS, HIDDEN], U8, align_bytes=64)
         planes_h = keep.tile([P, SLOTS, HIDDEN], U8, align_bytes=64)
         nc.vector.memset(planes_r[:].bitcast(I32), 0)
+        nc.vector.memset(planes_z[:].bitcast(I32), 0)
+        nc.vector.memset(planes_h[:].bitcast(I32), 0)
 
         bias_rows = keep.tile([P, 3 * HIDDEN], BF16)
         nc.vector.memset(bias_rows[:], 0.0)
@@ -121,8 +119,12 @@ def tile_grucell_k_kernel(
         ones = keep.tile([P, P], BF16)
         nc.vector.memset(ones[:], 1.0)
 
-        nc.vector.memset(planes_z[:].bitcast(I32), 0)
-        nc.vector.memset(planes_h[:].bitcast(I32), 0)
+        for q in range(BLOCKS_PER_PASS):
+            load_scale_row(nc.gpsimd, F32, planes_z, W_z_scales, q)
+        for q in range(BLOCKS_PER_PASS):
+            load_scale_row(nc.gpsimd, F32, planes_h, W_h_scales, q)
+        ident_bf16 = keep.tile([P, P], BF16)
+        make_identity(nc, ident_bf16[:])
 
         part_k = PASSES_PER_ROUND * K_PASS
         rows_per_part = BLOCKS_PER_PASS // ROUNDS
@@ -136,7 +138,7 @@ def tile_grucell_k_kernel(
             if from_inputs < part_k:
                 nc.sync.dma_start(out=part[:, from_inputs:part_k], in_=h_prev)
             for q in range(i * rows_per_part, (i + 1) * rows_per_part):
-                load_scale_row(nc, planes_r, W_r_scales, q)
+                load_scale_row(nc.sync, I32, planes_r, W_r_scales, q)
             ih_parts.append(part)
         h = ih_parts[ROUNDS - 1][:, part_k - HIDDEN : part_k]
 
@@ -196,15 +198,7 @@ def tile_grucell_k_kernel(
 
         acc_r = psum_acc.tile([P, HIDDEN], F32)
         gate_matmul(
-            nc,
-            w_pool,
-            acc_r,
-            W_r_words,
-            planes_r,
-            ih_codes_by_pass,
-            ih_scales_by_pass,
-            planes_z,
-            W_z_scales,
+            nc, w_pool, acc_r, W_r_words, planes_r, ih_codes_by_pass, ih_scales_by_pass, False
         )
         r = keep.tile([P, HIDDEN], F32)
         hard_sigmoid(nc, r, acc_r, offset_r)
@@ -219,15 +213,7 @@ def tile_grucell_k_kernel(
 
         acc_z = psum_acc.tile([P, HIDDEN], F32)
         gate_matmul(
-            nc,
-            w_pool,
-            acc_z,
-            W_z_words,
-            planes_z,
-            ih_codes_by_pass,
-            ih_scales_by_pass,
-            planes_h,
-            W_h_scales,
+            nc, w_pool, acc_z, W_z_words, planes_z, ih_codes_by_pass, ih_scales_by_pass, False
         )
         z = keep.tile([P, HIDDEN], F32)
         hard_sigmoid(nc, z, acc_z, offset_z)
@@ -260,14 +246,22 @@ def tile_grucell_k_kernel(
             planes_h,
             ih_codes_by_pass[: PASSES - 1] + [rh_codes[:]],
             ih_scales_by_pass[: PASSES - 1] + [rh_scales[:]],
-            None,
-            None,
+            True,
         )
         y = keep.tile([P, HIDDEN], F32)
-        nc.vector.tensor_tensor(out=y[:], in0=acc_h[:], in1=bias_h[:], op=ALU.add)
-        nc.vector.tensor_scalar(
-            out=y[:], in0=y[:], scalar1=-1.0, scalar2=1.0, op0=ALU.max, op1=ALU.min
-        )
-        nc.vector.tensor_tensor(out=y[:], in0=y[:], in1=one_minus_z[:], op=ALU.mult)
-        nc.vector.tensor_tensor(out=y[:], in0=y[:], in1=zh[:], op=ALU.add)
-        nc.sync.dma_start(out=out, in_=y[:])
+        halves = (slice(0, HIDDEN // 2), slice(HIDDEN // 2, HIDDEN))
+        for cols in halves:
+            nc.vector.tensor_tensor(
+                out=y[:, cols], in0=acc_h[:, cols], in1=bias_h[:, cols], op=ALU.add
+            )
+        for cols in halves:
+            nc.vector.tensor_scalar(
+                out=y[:, cols], in0=y[:, cols], scalar1=-1.0, scalar2=1.0, op0=ALU.max, op1=ALU.min
+            )
+        for cols in halves:
+            nc.vector.tensor_tensor(
+                out=y[:, cols], in0=y[:, cols], in1=one_minus_z[:, cols], op=ALU.mult
+            )
+        for cols in halves:
+            nc.vector.tensor_tensor(out=y[:, cols], in0=y[:, cols], in1=zh[:, cols], op=ALU.add)
+            nc.sync.dma_start(out=out[:, cols], in_=y[:, cols])

@@ -120,6 +120,8 @@ def tile_grucell_k_kernel(
         nc.vector.memset(ones[:], 1.0)
 
         for q in range(BLOCKS_PER_PASS):
+            load_scale_row(nc.gpsimd, F32, planes_r, W_r_scales, q)
+        for q in range(BLOCKS_PER_PASS):
             load_scale_row(nc.gpsimd, F32, planes_z, W_z_scales, q)
         for q in range(BLOCKS_PER_PASS):
             load_scale_row(nc.gpsimd, F32, planes_h, W_h_scales, q)
@@ -127,7 +129,6 @@ def tile_grucell_k_kernel(
         make_identity(nc, ident_bf16[:])
 
         part_k = PASSES_PER_ROUND * K_PASS
-        rows_per_part = BLOCKS_PER_PASS // ROUNDS
         ih_parts = []
         for i in range(ROUNDS):
             part = ih_pool.tile([P, part_k], BF16, tag="ih")
@@ -137,8 +138,6 @@ def tile_grucell_k_kernel(
             )
             if from_inputs < part_k:
                 nc.sync.dma_start(out=part[:, from_inputs:part_k], in_=h_prev)
-            for q in range(i * rows_per_part, (i + 1) * rows_per_part):
-                load_scale_row(nc.sync, I32, planes_r, W_r_scales, q)
             ih_parts.append(part)
         h = ih_parts[ROUNDS - 1][:, part_k - HIDDEN : part_k]
 

@@ -43,27 +43,39 @@ def load_scale_row(queue, view, planes, scales, q):
     )
 
 
-def gate_matmul(nc, w_pool, acc, words, planes, act_codes, act_scales, fine_end):
+def gate_matmul(nc, w_pool, accs, words, planes, act_codes, act_scales, split_end):
     words_i32 = words.rearrange("g p n t -> p g (n t)").bitcast(I32)
-    load_sizes = [PASSES_PER_W_LOAD] * (PASSES // PASSES_PER_W_LOAD)
-    if fine_end:
-        load_sizes = load_sizes[:-1] + [1] * PASSES_PER_W_LOAD
-    first = 0
-    for size in load_sizes:
-        w = w_pool.tile([P, size, HIDDEN], U32, tag="w", align_bytes=64)
-        nc.sync.dma_start(out=w[:].bitcast(I32), in_=words_i32[:, first : first + size, :])
+    width = HIDDEN // len(accs)
+
+    def load_and_multiply(first, size, parts):
+        n0, n1 = parts.start * width, parts.stop * width
+        w = w_pool.tile([P, size, n1 - n0], U32, tag="w", align_bytes=64)
+        nc.sync.dma_start(out=w[:].bitcast(I32), in_=words_i32[:, first : first + size, n0:n1])
         for j in range(size):
             g = first + j
-            nc.tensor.matmul_mx(
-                out=acc[:],
-                lhsT=act_codes[g].bitcast(FP8X4),
-                lhsT_scale=act_scales[g],
-                rhs=w[:, j, :].bitcast(FP8X4),
-                rhs_scale=planes[4 * (g // SLOTS) : P, g % SLOTS, :],
-                start=(g == 0),
-                stop=(g == PASSES - 1),
-            )
-        first += size
+            for i in range(parts.start, parts.stop):
+                cols = slice(i * width, (i + 1) * width)
+                w_cols = slice(i * width - n0, (i + 1) * width - n0)
+                nc.tensor.matmul_mx(
+                    out=accs[i][:],
+                    lhsT=act_codes[g].bitcast(FP8X4),
+                    lhsT_scale=act_scales[g],
+                    rhs=w[:, j, w_cols].bitcast(FP8X4),
+                    rhs_scale=planes[4 * (g // SLOTS) : P, g % SLOTS, cols],
+                    start=(g == 0),
+                    stop=(g == PASSES - 1),
+                )
+
+    everything = slice(0, len(accs))
+    whole_end = PASSES - PASSES_PER_W_LOAD if split_end else PASSES
+    for first in range(0, whole_end, PASSES_PER_W_LOAD):
+        load_and_multiply(first, PASSES_PER_W_LOAD, everything)
+    if split_end:
+        last = len(accs) - 1
+        for i in range(last):
+            load_and_multiply(whole_end, PASSES_PER_W_LOAD, slice(i, i + 1))
+        for g in range(whole_end, PASSES):
+            load_and_multiply(g, 1, slice(last, last + 1))
 
 
 def hard_sigmoid(nc, gate, acc, offset):
@@ -97,7 +109,7 @@ def tile_grucell_k_kernel(
         stage = ctx.enter_context(tc.tile_pool(name="stage", bufs=3))
         w_pool = ctx.enter_context(tc.tile_pool(name="weights", bufs=W_BUFFERS))
         psum_t = ctx.enter_context(tc.psum_pool(name="psum_t", bufs=3))
-        psum_b = ctx.enter_context(tc.psum_pool(name="psum_b", bufs=2))
+        psum_b = ctx.enter_context(tc.psum_pool(name="psum_b", bufs=1))
         psum_acc = ctx.enter_context(tc.psum_pool(name="psum_acc", bufs=1))
 
         ident_f32 = keep.tile([P, P], F32)
@@ -197,7 +209,7 @@ def tile_grucell_k_kernel(
 
         acc_r = psum_acc.tile([P, HIDDEN], F32)
         gate_matmul(
-            nc, w_pool, acc_r, W_r_words, planes_r, ih_codes_by_pass, ih_scales_by_pass, False
+            nc, w_pool, [acc_r], W_r_words, planes_r, ih_codes_by_pass, ih_scales_by_pass, False
         )
         r = keep.tile([P, HIDDEN], F32)
         hard_sigmoid(nc, r, acc_r, offset_r)
@@ -212,7 +224,7 @@ def tile_grucell_k_kernel(
 
         acc_z = psum_acc.tile([P, HIDDEN], F32)
         gate_matmul(
-            nc, w_pool, acc_z, W_z_words, planes_z, ih_codes_by_pass, ih_scales_by_pass, False
+            nc, w_pool, [acc_z], W_z_words, planes_z, ih_codes_by_pass, ih_scales_by_pass, False
         )
         z = keep.tile([P, HIDDEN], F32)
         hard_sigmoid(nc, z, acc_z, offset_z)
@@ -236,11 +248,13 @@ def tile_grucell_k_kernel(
             in_=rh_grouped[:].rearrange("p b t -> p (b t)"),
         )
 
-        acc_h = psum_acc.tile([P, HIDDEN], F32)
+        half = HIDDEN // 2
+        acc_h0 = psum_acc.tile([P, half], F32)
+        acc_h1 = psum_acc.tile([P, half], F32)
         gate_matmul(
             nc,
             w_pool,
-            acc_h,
+            [acc_h0, acc_h1],
             W_h_words,
             planes_h,
             ih_codes_by_pass[: PASSES - 1] + [rh_codes[:]],
@@ -248,19 +262,33 @@ def tile_grucell_k_kernel(
             True,
         )
         y = keep.tile([P, HIDDEN], F32)
-        halves = (slice(0, HIDDEN // 2), slice(HIDDEN // 2, HIDDEN))
-        for cols in halves:
-            nc.vector.tensor_tensor(
-                out=y[:, cols], in0=acc_h[:, cols], in1=bias_h[:, cols], op=ALU.add
+        quarter = HIDDEN // 4
+        for acc, start in ((acc_h0, 0), (acc_h1, half)):
+            quarters = [slice(start + i * quarter, start + (i + 1) * quarter) for i in range(2)]
+            for i, cols in enumerate(quarters):
+                nc.vector.tensor_tensor(
+                    out=y[:, cols],
+                    in0=acc[:, i * quarter : (i + 1) * quarter],
+                    in1=bias_h[:, cols],
+                    op=ALU.add,
+                )
+            for cols in quarters:
+                nc.vector.tensor_scalar(
+                    out=y[:, cols],
+                    in0=y[:, cols],
+                    scalar1=-1.0,
+                    scalar2=1.0,
+                    op0=ALU.max,
+                    op1=ALU.min,
+                )
+            for cols in quarters:
+                nc.vector.tensor_tensor(
+                    out=y[:, cols], in0=y[:, cols], in1=one_minus_z[:, cols], op=ALU.mult
+                )
+            for cols in quarters:
+                nc.vector.tensor_tensor(
+                    out=y[:, cols], in0=y[:, cols], in1=zh[:, cols], op=ALU.add
+                )
+            nc.sync.dma_start(
+                out=out[:, start : start + half], in_=y[:, start : start + half]
             )
-        for cols in halves:
-            nc.vector.tensor_scalar(
-                out=y[:, cols], in0=y[:, cols], scalar1=-1.0, scalar2=1.0, op0=ALU.max, op1=ALU.min
-            )
-        for cols in halves:
-            nc.vector.tensor_tensor(
-                out=y[:, cols], in0=y[:, cols], in1=one_minus_z[:, cols], op=ALU.mult
-            )
-        for cols in halves:
-            nc.vector.tensor_tensor(out=y[:, cols], in0=y[:, cols], in1=zh[:, cols], op=ALU.add)
-            nc.sync.dma_start(out=out[:, cols], in_=y[:, cols])

@@ -25,12 +25,16 @@ PASSES_PER_BANK = 2
 BANKS_PER_ROUND = 2
 PASSES_PER_ROUND = PASSES_PER_BANK * BANKS_PER_ROUND
 ROUNDS = PASSES // PASSES_PER_ROUND
+PASSES_PER_PART = 8
+PARTS = PASSES // PASSES_PER_PART
+ROUNDS_PER_PART = PASSES_PER_PART // PASSES_PER_ROUND
 PASSES_PER_W_LOAD = 4
 W_BUFFERS = 12
 
 PLANES_PER_TILE = 4
 SLOTS = PASSES // PLANES_PER_TILE
 BLOCKS_PER_PASS = K_PASS // 32
+ROWS_ON_SCALAR = 4
 
 FLOPS = 3 * 2 * BATCH * FEATURES * HIDDEN
 
@@ -41,6 +45,17 @@ def load_scale_row(queue, view, planes, scales, q):
         out=planes[32 * quadrant + r : 32 * quadrant + 4 * PLANES_PER_TILE : 4, :, :].bitcast(view),
         in_=scales.bitcast(view)[:, q, :].rearrange("(o s) n -> o s n", o=PLANES_PER_TILE),
     )
+
+
+def in_turns(rows):
+    n = len(rows) // 4
+    low = [q for q in rows if q < BLOCKS_PER_PASS // 2]
+    high = [q for q in rows if q >= BLOCKS_PER_PASS // 2]
+    left = low[n:] + high[n:]
+    order = []
+    for turns in zip(low[:n], left[:n], high[:n], left[n:]):
+        order.extend(turns)
+    return order
 
 
 def gate_matmul(nc, w_pool, accs, words, planes, act_codes, act_scales, split_end):
@@ -105,7 +120,7 @@ def tile_grucell_k_kernel(
     nc = tc.nc
     with ExitStack() as ctx:
         keep = ctx.enter_context(tc.tile_pool(name="keep", bufs=1))
-        ih_pool = ctx.enter_context(tc.tile_pool(name="ih", bufs=ROUNDS))
+        ih_pool = ctx.enter_context(tc.tile_pool(name="ih", bufs=PARTS))
         stage = ctx.enter_context(tc.tile_pool(name="stage", bufs=3))
         w_pool = ctx.enter_context(tc.tile_pool(name="weights", bufs=W_BUFFERS))
         psum_t = ctx.enter_context(tc.psum_pool(name="psum_t", bufs=3))
@@ -131,18 +146,19 @@ def tile_grucell_k_kernel(
         ones = keep.tile([P, P], BF16)
         nc.vector.memset(ones[:], 1.0)
 
-        for q in range(BLOCKS_PER_PASS):
+        for q in range(ROWS_ON_SCALAR):
+            load_scale_row(nc.scalar, F32, planes_r, W_r_scales, q)
+        for q in in_turns(range(ROWS_ON_SCALAR, BLOCKS_PER_PASS)):
             load_scale_row(nc.gpsimd, F32, planes_r, W_r_scales, q)
-        for q in range(BLOCKS_PER_PASS):
-            load_scale_row(nc.gpsimd, F32, planes_z, W_z_scales, q)
-        for q in range(BLOCKS_PER_PASS):
-            load_scale_row(nc.gpsimd, F32, planes_h, W_h_scales, q)
+        for planes, scales in ((planes_z, W_z_scales), (planes_h, W_h_scales)):
+            for q in in_turns(range(BLOCKS_PER_PASS)):
+                load_scale_row(nc.gpsimd, F32, planes, scales, q)
         ident_bf16 = keep.tile([P, P], BF16)
         make_identity(nc, ident_bf16[:])
 
-        part_k = PASSES_PER_ROUND * K_PASS
+        part_k = PASSES_PER_PART * K_PASS
         ih_parts = []
-        for i in range(ROUNDS):
+        for i in range(PARTS):
             part = ih_pool.tile([P, part_k], BF16, tag="ih")
             from_inputs = min(part_k, IN_FEATURES - i * part_k)
             nc.sync.dma_start(
@@ -151,7 +167,7 @@ def tile_grucell_k_kernel(
             if from_inputs < part_k:
                 nc.sync.dma_start(out=part[:, from_inputs:part_k], in_=h_prev)
             ih_parts.append(part)
-        h = ih_parts[ROUNDS - 1][:, part_k - HIDDEN : part_k]
+        h = ih_parts[PARTS - 1][:, part_k - HIDDEN : part_k]
 
         offset_r = keep.tile([P, HIDDEN], F32)
         offset_z = keep.tile([P, HIDDEN], F32)
@@ -178,7 +194,8 @@ def tile_grucell_k_kernel(
         ih_codes = keep.tile([P, PASSES * BATCH], U32, align_bytes=64)
         ih_scales = keep.tile([P, PASSES * BATCH], U8, align_bytes=64)
         for rnd in range(ROUNDS):
-            ih_pairs = ih_parts[rnd][:].bitcast(F32)
+            ih_pairs = ih_parts[rnd // ROUNDS_PER_PART][:].bitcast(F32)
+            first = rnd % ROUNDS_PER_PART * PASSES_PER_ROUND
             grouped = stage.tile([P, PASSES_PER_ROUND * BATCH * PACK], BF16, align_bytes=64)
             grouped_pairs = (
                 grouped[:].bitcast(F32).rearrange("p (g b u) -> p g b u", g=PASSES_PER_ROUND, u=2)
@@ -186,7 +203,7 @@ def tile_grucell_k_kernel(
             for bank in range(BANKS_PER_ROUND):
                 pairs_t = psum_t.tile([P, PASSES_PER_BANK, 2, BATCH], F32, tag="transposed")
                 for i in range(PASSES_PER_BANK):
-                    g = bank * PASSES_PER_BANK + i
+                    g = first + bank * PASSES_PER_BANK + i
                     for u in range(2):
                         nc.tensor.transpose(
                             pairs_t[:, i, u, :],

@@ -28,8 +28,9 @@ ROUNDS = PASSES // PASSES_PER_ROUND
 PASSES_PER_PART = 8
 PARTS = PASSES // PASSES_PER_PART
 ROUNDS_PER_PART = PASSES_PER_PART // PASSES_PER_ROUND
-PASSES_PER_W_LOAD = 4
-W_BUFFERS = 12
+PASSES_PER_W_LOAD = 8
+W_BUFFERS = 7
+END_PASSES = 4
 
 PLANES_PER_TILE = 4
 SLOTS = PASSES // PLANES_PER_TILE
@@ -82,13 +83,13 @@ def gate_matmul(nc, w_pool, accs, words, planes, act_codes, act_scales, split_en
                 )
 
     everything = slice(0, len(accs))
-    whole_end = PASSES - PASSES_PER_W_LOAD if split_end else PASSES
+    whole_end = PASSES - END_PASSES if split_end else PASSES
     for first in range(0, whole_end, PASSES_PER_W_LOAD):
-        load_and_multiply(first, PASSES_PER_W_LOAD, everything)
+        load_and_multiply(first, min(PASSES_PER_W_LOAD, whole_end - first), everything)
     if split_end:
         last = len(accs) - 1
         for i in range(last):
-            load_and_multiply(whole_end, PASSES_PER_W_LOAD, slice(i, i + 1))
+            load_and_multiply(whole_end, END_PASSES, slice(i, i + 1))
         for g in range(whole_end, PASSES):
             load_and_multiply(g, 1, slice(last, last + 1))
 
@@ -134,11 +135,11 @@ def tile_grucell_k_kernel(
         planes_z = keep.tile([P, SLOTS, HIDDEN], U8, align_bytes=64)
         planes_h = keep.tile([P, SLOTS, HIDDEN], U8, align_bytes=64)
         nc.vector.memset(planes_r[:].bitcast(I32), 0)
+        bias_rows = keep.tile([P, 3 * HIDDEN], BF16)
+        nc.vector.memset(bias_rows[:], 0.0)
         nc.vector.memset(planes_z[:].bitcast(I32), 0)
         nc.vector.memset(planes_h[:].bitcast(I32), 0)
 
-        bias_rows = keep.tile([P, 3 * HIDDEN], BF16)
-        nc.vector.memset(bias_rows[:], 0.0)
         for i, bias in enumerate((b_r, b_z, b_h)):
             nc.scalar.dma_start(
                 out=bias_rows[0:1, i * HIDDEN : (i + 1) * HIDDEN], in_=bias.unsqueeze(0)
@@ -161,11 +162,11 @@ def tile_grucell_k_kernel(
         for i in range(PARTS):
             part = ih_pool.tile([P, part_k], BF16, tag="ih")
             from_inputs = min(part_k, IN_FEATURES - i * part_k)
-            nc.sync.dma_start(
+            nc.scalar.dma_start(
                 out=part[:, 0:from_inputs], in_=inputs[:, i * part_k : i * part_k + from_inputs]
             )
             if from_inputs < part_k:
-                nc.sync.dma_start(out=part[:, from_inputs:part_k], in_=h_prev)
+                nc.scalar.dma_start(out=part[:, from_inputs:part_k], in_=h_prev)
             ih_parts.append(part)
         h = ih_parts[PARTS - 1][:, part_k - HIDDEN : part_k]
 

from contextlib import ExitStack

import concourse.mybir as mybir
from concourse.masks import make_identity

F32 = mybir.dt.float32
BF16 = mybir.dt.bfloat16
I32 = mybir.dt.int32
U32 = mybir.dt.uint32
U8 = mybir.dt.uint8
FP8X4 = mybir.dt.float8_e4m3fn_x4
ALU = mybir.AluOpType

P = 128
PACK = 4
K_PASS = P * PACK
BATCH = 128
IN_FEATURES = 15872
HIDDEN = 512
FEATURES = IN_FEATURES + HIDDEN
PASSES = FEATURES // K_PASS
PAIRS_PER_PASS = K_PASS // 2

PASSES_PER_BANK = 2
BANKS_PER_ROUND = 2
PASSES_PER_ROUND = PASSES_PER_BANK * BANKS_PER_ROUND
ROUNDS = PASSES // PASSES_PER_ROUND
PASSES_PER_PART = 8
PARTS = PASSES // PASSES_PER_PART
ROUNDS_PER_PART = PASSES_PER_PART // PASSES_PER_ROUND
PASSES_PER_W_LOAD = 8
W_BUFFERS = 7
END_PASSES = 4

PLANES_PER_TILE = 4
SLOTS = PASSES // PLANES_PER_TILE
BLOCKS_PER_PASS = K_PASS // 32
ROWS_ON_SCALAR = 4

FLOPS = 3 * 2 * BATCH * FEATURES * HIDDEN


def load_scale_row(queue, view, planes, scales, q):
    quadrant, r = divmod(q, 4)
    queue.dma_start(
        out=planes[32 * quadrant + r : 32 * quadrant + 4 * PLANES_PER_TILE : 4, :, :].bitcast(view),
        in_=scales.bitcast(view)[:, q, :].rearrange("(o s) n -> o s n", o=PLANES_PER_TILE),
    )


def in_turns(rows):
    n = len(rows) // 4
    low = [q for q in rows if q < BLOCKS_PER_PASS // 2]
    high = [q for q in rows if q >= BLOCKS_PER_PASS // 2]
    left = low[n:] + high[n:]
    order = []
    for turns in zip(low[:n], left[:n], high[:n], left[n:]):
        order.extend(turns)
    return order


def gate_matmul(nc, w_pool, accs, words, planes, act_codes, act_scales, split_end):
    words_i32 = words.rearrange("g p n t -> p g (n t)").bitcast(I32)
    width = HIDDEN // len(accs)

    def load_and_multiply(first, size, parts):
        n0, n1 = parts.start * width, parts.stop * width
        w = w_pool.tile([P, size, n1 - n0], U32, tag="w", align_bytes=64)
        nc.sync.dma_start(out=w[:].bitcast(I32), in_=words_i32[:, first : first + size, n0:n1])
        for j in range(size):
            g = first + j
            for i in range(parts.start, parts.stop):
                cols = slice(i * width, (i + 1) * width)
                w_cols = slice(i * width - n0, (i + 1) * width - n0)
                nc.tensor.matmul_mx(
                    out=accs[i][:],
                    lhsT=act_codes[g].bitcast(FP8X4),
                    lhsT_scale=act_scales[g],
                    rhs=w[:, j, w_cols].bitcast(FP8X4),
                    rhs_scale=planes[4 * (g // SLOTS) : P, g % SLOTS, cols],
                    start=(g == 0),
                    stop=(g == PASSES - 1),
                )

    everything = slice(0, len(accs))
    whole_end = PASSES - END_PASSES if split_end else PASSES
    for first in range(0, whole_end, PASSES_PER_W_LOAD):
        load_and_multiply(first, min(PASSES_PER_W_LOAD, whole_end - first), everything)
    if split_end:
        last = len(accs) - 1
        for i in range(last):
            load_and_multiply(whole_end, END_PASSES, slice(i, i + 1))
        for g in range(whole_end, PASSES):
            load_and_multiply(g, 1, slice(last, last + 1))


def hard_sigmoid(nc, gate, acc, offset):
    nc.vector.scalar_tensor_tensor(
        out=gate[:], in0=acc[:], scalar=1.0 / 6.0, in1=offset[:], op0=ALU.mult, op1=ALU.add
    )
    nc.vector.tensor_scalar(
        out=gate[:], in0=gate[:], scalar1=0.0, scalar2=1.0, op0=ALU.max, op1=ALU.min
    )


def tile_grucell_k_kernel(
    tc,
    inputs,
    h_prev,
    W_z_words,
    W_z_scales,
    b_z,
    W_r_words,
    W_r_scales,
    b_r,
    W_h_words,
    W_h_scales,
    b_h,
    out,
):
    nc = tc.nc
    with ExitStack() as ctx:
        keep = ctx.enter_context(tc.tile_pool(name="keep", bufs=1))
        ih_pool = ctx.enter_context(tc.tile_pool(name="ih", bufs=PARTS))
        stage = ctx.enter_context(tc.tile_pool(name="stage", bufs=3))
        w_pool = ctx.enter_context(tc.tile_pool(name="weights", bufs=W_BUFFERS))
        psum_t = ctx.enter_context(tc.psum_pool(name="psum_t", bufs=3))
        psum_b = ctx.enter_context(tc.psum_pool(name="psum_b", bufs=1))
        psum_acc = ctx.enter_context(tc.psum_pool(name="psum_acc", bufs=1))

        ident_f32 = keep.tile([P, P], F32)
        make_identity(nc, ident_f32[:])

        planes_r = keep.tile([P, SLOTS, HIDDEN], U8, align_bytes=64)
        planes_z = keep.tile([P, SLOTS, HIDDEN], U8, align_bytes=64)
        planes_h = keep.tile([P, SLOTS, HIDDEN], U8, align_bytes=64)
        nc.vector.memset(planes_r[:].bitcast(I32), 0)
        bias_rows = keep.tile([P, 3 * HIDDEN], BF16)
        nc.vector.memset(bias_rows[:], 0.0)
        nc.vector.memset(planes_z[:].bitcast(I32), 0)
        nc.vector.memset(planes_h[:].bitcast(I32), 0)

        for i, bias in enumerate((b_r, b_z, b_h)):
            nc.scalar.dma_start(
                out=bias_rows[0:1, i * HIDDEN : (i + 1) * HIDDEN], in_=bias.unsqueeze(0)
            )
        ones = keep.tile([P, P], BF16)
        nc.vector.memset(ones[:], 1.0)

        for q in range(ROWS_ON_SCALAR):
            load_scale_row(nc.scalar, F32, planes_r, W_r_scales, q)
        for q in in_turns(range(ROWS_ON_SCALAR, BLOCKS_PER_PASS)):
            load_scale_row(nc.gpsimd, F32, planes_r, W_r_scales, q)
        for planes, scales in ((planes_z, W_z_scales), (planes_h, W_h_scales)):
            for q in in_turns(range(BLOCKS_PER_PASS)):
                load_scale_row(nc.gpsimd, F32, planes, scales, q)
        ident_bf16 = keep.tile([P, P], BF16)
        make_identity(nc, ident_bf16[:])

        part_k = PASSES_PER_PART * K_PASS
        ih_parts = []
        for i in range(PARTS):
            part = ih_pool.tile([P, part_k], BF16, tag="ih")
            from_inputs = min(part_k, IN_FEATURES - i * part_k)
            nc.scalar.dma_start(
                out=part[:, 0:from_inputs], in_=inputs[:, i * part_k : i * part_k + from_inputs]
            )
            if from_inputs < part_k:
                nc.scalar.dma_start(out=part[:, from_inputs:part_k], in_=h_prev)
            ih_parts.append(part)
        h = ih_parts[PARTS - 1][:, part_k - HIDDEN : part_k]

        offset_r = keep.tile([P, HIDDEN], F32)
        offset_z = keep.tile([P, HIDDEN], F32)
        bias_h = keep.tile([P, HIDDEN], F32)
        spreads = ((offset_r, 1.0 / 6.0, 0.5), (offset_z, 1.0 / 6.0, 0.5), (bias_h, 1.0, 0.0))
        for i, (spread, factor, shift) in enumerate(spreads):
            bias_ps = psum_b.tile([P, HIDDEN], F32)
            nc.tensor.matmul(
                bias_ps[:],
                lhsT=ones[:],
                rhs=bias_rows[:, i * HIDDEN : (i + 1) * HIDDEN],
                start=True,
                stop=True,
            )
            nc.vector.tensor_scalar(
                out=spread[:],
                in0=bias_ps[:],
                scalar1=factor,
                scalar2=shift,
                op0=ALU.mult,
                op1=ALU.add,
            )

        ih_codes = keep.tile([P, PASSES * BATCH], U32, align_bytes=64)
        ih_scales = keep.tile([P, PASSES * BATCH], U8, align_bytes=64)
        for rnd in range(ROUNDS):
            ih_pairs = ih_parts[rnd // ROUNDS_PER_PART][:].bitcast(F32)
            first = rnd % ROUNDS_PER_PART * PASSES_PER_ROUND
            grouped = stage.tile([P, PASSES_PER_ROUND * BATCH * PACK], BF16, align_bytes=64)
            grouped_pairs = (
                grouped[:].bitcast(F32).rearrange("p (g b u) -> p g b u", g=PASSES_PER_ROUND, u=2)
            )
            for bank in range(BANKS_PER_ROUND):
                pairs_t = psum_t.tile([P, PASSES_PER_BANK, 2, BATCH], F32, tag="transposed")
                for i in range(PASSES_PER_BANK):
                    g = first + bank * PASSES_PER_BANK + i
                    for u in range(2):
                        nc.tensor.transpose(
                            pairs_t[:, i, u, :],
                            ih_pairs[:, PAIRS_PER_PASS * g + u : PAIRS_PER_PASS * (g + 1) : 2],
                            ident_f32[:],
                        )
                copy = nc.vector.tensor_copy if bank % 2 == 0 else nc.scalar.copy
                copy(
                    out=grouped_pairs[
                        :, bank * PASSES_PER_BANK : (bank + 1) * PASSES_PER_BANK, :, :
                    ],
                    in_=pairs_t[:].rearrange("p g u b -> p g b u"),
                )
            cols = slice(rnd * PASSES_PER_ROUND * BATCH, (rnd + 1) * PASSES_PER_ROUND * BATCH)
            nc.vector.quantize_mx(
                out=ih_codes[:, cols].bitcast(FP8X4), scales=ih_scales[:, cols], in_=grouped[:]
            )
        ih_codes_by_pass = [ih_codes[:, g * BATCH : (g + 1) * BATCH] for g in range(PASSES)]
        ih_scales_by_pass = [ih_scales[:, g * BATCH : (g + 1) * BATCH] for g in range(PASSES)]

        acc_r = psum_acc.tile([P, HIDDEN], F32)
        gate_matmul(
            nc, w_pool, [acc_r], W_r_words, planes_r, ih_codes_by_pass, ih_scales_by_pass, False
        )
        r = keep.tile([P, HIDDEN], F32)
        hard_sigmoid(nc, r, acc_r, offset_r)

        rh_sorted = keep.tile([P, PACK, P], BF16)
        nc.vector.tensor_tensor(
            out=rh_sorted[:],
            in0=r[:].rearrange("b (p t) -> b t p", t=PACK),
            in1=h.rearrange("b (p t) -> b t p", t=PACK),
            op=ALU.mult,
        )

        acc_z = psum_acc.tile([P, HIDDEN], F32)
        gate_matmul(
            nc, w_pool, [acc_z], W_z_words, planes_z, ih_codes_by_pass, ih_scales_by_pass, False
        )
        z = keep.tile([P, HIDDEN], F32)
        hard_sigmoid(nc, z, acc_z, offset_z)
        zh = keep.tile([P, HIDDEN], F32)
        nc.vector.tensor_tensor(out=zh[:], in0=z[:], in1=h, op=ALU.mult)
        one_minus_z = keep.tile([P, HIDDEN], F32)
        nc.vector.tensor_scalar(
            out=one_minus_z[:], in0=z[:], scalar1=-1.0, scalar2=1.0, op0=ALU.mult, op1=ALU.add
        )

        rh_t = psum_t.tile([P, PACK, BATCH], BF16, tag="transposed")
        for t in range(PACK):
            nc.tensor.transpose(rh_t[:, t, :], rh_sorted[:, t, :], ident_bf16[:])
        rh_grouped = keep.tile([P, BATCH, PACK], BF16, align_bytes=64)
        nc.vector.tensor_copy(out=rh_grouped[:], in_=rh_t[:].rearrange("p t b -> p b t"))
        rh_codes = keep.tile([P, BATCH], U32, align_bytes=64)
        rh_scales = keep.tile([P, BATCH], U8, align_bytes=64)
        nc.vector.quantize_mx(
            out=rh_codes[:].bitcast(FP8X4),
            scales=rh_scales[:],
            in_=rh_grouped[:].rearrange("p b t -> p (b t)"),
        )

        half = HIDDEN // 2
        acc_h0 = psum_acc.tile([P, half], F32)
        acc_h1 = psum_acc.tile([P, half], F32)
        gate_matmul(
            nc,
            w_pool,
            [acc_h0, acc_h1],
            W_h_words,
            planes_h,
            ih_codes_by_pass[: PASSES - 1] + [rh_codes[:]],
            ih_scales_by_pass[: PASSES - 1] + [rh_scales[:]],
            True,
        )
        y = keep.tile([P, HIDDEN], F32)
        quarter = HIDDEN // 4
        for acc, start in ((acc_h0, 0), (acc_h1, half)):
            quarters = [slice(start + i * quarter, start + (i + 1) * quarter) for i in range(2)]
            for i, cols in enumerate(quarters):
                nc.vector.tensor_tensor(
                    out=y[:, cols],
                    in0=acc[:, i * quarter : (i + 1) * quarter],
                    in1=bias_h[:, cols],
                    op=ALU.add,
                )
            for cols in quarters:
                nc.vector.tensor_scalar(
                    out=y[:, cols],
                    in0=y[:, cols],
                    scalar1=-1.0,
                    scalar2=1.0,
                    op0=ALU.max,
                    op1=ALU.min,
                )
            for cols in quarters:
                nc.vector.tensor_tensor(
                    out=y[:, cols], in0=y[:, cols], in1=one_minus_z[:, cols], op=ALU.mult
                )
            for cols in quarters:
                nc.vector.tensor_tensor(
                    out=y[:, cols], in0=y[:, cols], in1=zh[:, cols], op=ALU.add
                )
            nc.sync.dma_start(
                out=out[:, start : start + half], in_=y[:, start : start + half]
            )
